import numpy as np
import ml_dtypes


def mxq(x, axis, fmt="e4m3"):
    dtype, down = {"e4m3": (ml_dtypes.float8_e4m3fn, 7), "e5m2": (ml_dtypes.float8_e5m2, 14)}[fmt]
    v = np.moveaxis(np.asarray(x, np.float32).astype(ml_dtypes.bfloat16).astype(np.float64), axis, -1)
    blocks = v.reshape(v.shape[:-1] + (-1, 32))
    amax = np.abs(blocks).max(-1, keepdims=True)
    byte = np.maximum(np.where(amax > 0, np.frexp(amax)[1] - 1 + 127, 0) - down, 1)
    scale = np.exp2(byte - 127.0)
    codes = (blocks / scale).astype(np.float32).astype(dtype).astype(np.float64)
    return np.moveaxis((codes * scale).reshape(v.shape), -1, axis)


WIDE = False


def mx_kscale(k):
    if not WIDE:
        return np.ones(k)
    levels = np.array([10, -10, 5, -5, 0])
    a = np.random.permutation(np.resize(levels, k // 512 * 4)).reshape(k // 512, 4)
    idx = np.arange(k)
    return np.exp2(a[idx // 512, idx % 128 // 32])


BF16 = ml_dtypes.bfloat16


def bf(x):
    return np.asarray(x, np.float32).astype(BF16)


def f64(x):
    return np.asarray(x).astype(np.float64)


NS, NI, T = 384, 128, 8193
NA = NS + NI


def setup_inputs():
    s = mx_kscale(NA)
    r = s[:NS]
    A = np.random.standard_normal((NS, NS)) / np.sqrt(NA)
    B = np.random.standard_normal((NS, NI)) / np.sqrt(NA)
    x0 = np.random.standard_normal(NS) * 3.0
    V = np.random.standard_normal((T, NA))
    V[0, :NS] *= 3.0
    return {"A": bf(A * r[:, None] / s[None, :NS]), "B": bf(B * r[:, None] / s[None, NS:]), "x0": bf(x0 * r),
            "net_input": bf((V * s[None, :]).reshape(-1)), "T": T}


def reference(A, B, x0, net_input, T):
    n_state = A.shape[0]
    n_all = n_state + B.shape[1]
    AB = np.concatenate([f64(A), f64(B)], axis=1)
    V = f64(net_input).reshape(T, n_all)
    out0 = V[0, :n_state] - f64(x0)
    prop = mxq(V[:-1], 1, "e4m3") @ mxq(AB, 1, "e4m3").T
    out_rest = prop - V[1:, :n_state]
    return np.concatenate([out0, out_rest.reshape(-1)])

@@ -1,0 +1,146 @@
+from contextlib import ExitStack
+
+import concourse.mybir as mybir
+from concourse.masks import make_identity
+
+F32 = mybir.dt.float32
+BF16 = mybir.dt.bfloat16
+U32 = mybir.dt.uint32
+U8 = mybir.dt.uint8
+FP8X4 = mybir.dt.float8_e4m3fn_x4
+SUB = mybir.AluOpType.subtract
+
+P = 128
+NS = 384
+NA = 512
+STEPS = 8192
+J = STEPS // P
+GROUP = 4
+LOAD_CHUNKS = [4, 4, 8, 16, 16, 16]
+FLOPS = 2 * STEPS * NS * NA
+
+
+def tile_constrainnet_t_kernel(tc, A, B, x0, net_input, T, out):
+    nc = tc.nc
+    assert T == STEPS + 1
+    n_groups = J // GROUP
+    with ExitStack() as ctx:
+        const = ctx.enter_context(tc.tile_pool(name="const", bufs=1))
+        vpool = ctx.enter_context(tc.tile_pool(name="vpool", bufs=1))
+        opool = ctx.enter_context(tc.tile_pool(name="opool", bufs=1))
+        gpool = ctx.enter_context(tc.tile_pool(name="gpool", bufs=3))
+        qpool = ctx.enter_context(tc.tile_pool(name="qpool", bufs=3))
+        xt_ps = ctx.enter_context(tc.psum_pool(name="xt_ps", bufs=3))
+        pr_ps = ctx.enter_context(tc.psum_pool(name="pr_ps", bufs=5))
+
+        ident = const.tile([P, P], F32, name="ident")
+        make_identity(nc, ident[:])
+
+        ab_sb = const.tile([P, 3, NA], BF16, name="ab_sb")
+        nc.sync.dma_start(out=ab_sb[:, :, 0:NS], in_=A.rearrange("(r p) k -> p r k", p=P))
+        nc.sync.dma_start(out=ab_sb[:, :, NS:NA], in_=B.rearrange("(r p) k -> p r k", p=P))
+        v_rows = net_input[0 : STEPS * NA].rearrange("(p j k) -> p j k", p=P, j=J)
+        where = []
+        j0 = 0
+        for c, n in enumerate(LOAD_CHUNKS):
+            vt = vpool.tile([P, n, NA], BF16, name="v%d" % c)
+            nc.sync.dma_start(out=vt[:], in_=v_rows[:, j0 : j0 + n, :])
+            for i in range(n):
+                where.append((vt, i))
+            j0 += n
+        assert j0 == J
+        v_next = net_input[NA : (STEPS + 1) * NA].rearrange("(p j k) -> p j k", p=P, j=J)
+        v_last = vpool.tile([P, 1, NS], BF16, name="v_last")
+        nc.sync.dma_start(out=v_last[:], in_=v_next[:, J - 1 : J, 0:NS])
+        where.append((v_last, 0))
+        x0_sb = const.tile([1, NS], BF16, name="x0_sb")
+        nc.sync.dma_start(out=x0_sb[:], in_=x0.rearrange("(o n) -> o n", o=1))
+
+        out_rows = out[NS : (STEPS + 1) * NS].rearrange("(p j i) -> p j i", p=P, j=J)
+
+        def transpose_pair(srcs, dst_f32):
+            xt = xt_ps.tile([P, 4, P], F32, name="xt")
+            n = len(srcs)
+            for t, s in enumerate(srcs):
+                for u in range(2):
+                    nc.tensor.transpose(xt[:, 2 * t + u, :], s[:, u * P : (u + 1) * P], ident[:])
+            nc.scalar.copy(
+                out=dst_f32,
+                in_=xt[:, 0 : 2 * n, :].rearrange("q (t u) c -> q t c u", u=2),
+            )
+
+        ab_f = ab_sb[:].bitcast(F32)
+        ab_g = const.tile([P, NS * 4], BF16, name="ab_g", align_bytes=64)
+        ab_gf = ab_g[:].bitcast(F32).rearrange("q (t c u) -> q t c u", t=3, u=2)
+        ab_codes = const.tile([P, NS], U32, name="ab_codes", align_bytes=64)
+        ab_scales = const.tile([P, NS], U8, name="ab_scales", align_bytes=64)
+        transpose_pair([ab_f[:, 0, :], ab_f[:, 1, :]], ab_gf[:, 0:2, :, :])
+        transpose_pair([ab_f[:, 2, :]], ab_gf[:, 2:3, :, :])
+        nc.vector.quantize_mx(
+            out=ab_codes[:, 0:256].bitcast(FP8X4), scales=ab_scales[:, 0:256], in_=ab_g[:, 0:1024]
+        )
+        nc.vector.quantize_mx(
+            out=ab_codes[:, 256:384].bitcast(FP8X4), scales=ab_scales[:, 256:384], in_=ab_g[:, 1024:1536]
+        )
+
+        grouped = {}
+        quant = {}
+        prods = {}
+
+        def stage_t(g):
+            gr = gpool.tile([P, GROUP * 4 * P], BF16, name="gr", align_bytes=64)
+            grf = gr[:].bitcast(F32).rearrange("q (t c u) -> q t c u", t=GROUP, u=2)
+            for h in range(GROUP // 2):
+                srcs = []
+                for t in range(2):
+                    vt, i = where[g * GROUP + 2 * h + t]
+                    srcs.append(vt[:].bitcast(F32)[:, i, :])
+                transpose_pair(srcs, grf[:, 2 * h : 2 * h + 2, :, :])
+            grouped[g] = gr
+
+        def stage_q(g):
+            codes = qpool.tile([P, GROUP * P], U32, name="codes", align_bytes=64)
+            scales = qpool.tile([P, GROUP * P], U8, name="scales", align_bytes=64)
+            nc.vector.quantize_mx(out=codes[:].bitcast(FP8X4), scales=scales[:], in_=grouped[g][:])
+            quant[g] = (codes, scales)
+
+        def stage_m(g):
+            codes, scales = quant[g]
+            prods[g] = []
+            for t in range(GROUP):
+                pr = pr_ps.tile([P, 512], F32, name="pr")
+                cols = slice(t * P, (t + 1) * P)
+                for lo, hi in ((0, 256), (256, 384)):
+                    nc.tensor.matmul_mx(
+                        out=pr[:, lo:hi],
+                        lhsT=codes[:, cols].bitcast(FP8X4),
+                        lhsT_scale=scales[:, cols],
+                        rhs=ab_codes[:, lo:hi].bitcast(FP8X4),
+                        rhs_scale=ab_scales[:, lo:hi],
+                        start=True,
+                        stop=True,
+                    )
+                prods[g].append(pr)
+
+        def stage_s(g):
+            o = opool.tile([P, GROUP, NS], F32, name="o%d" % g)
+            for t in range(GROUP):
+                vt, i = where[g * GROUP + t + 1]
+                nc.vector.tensor_tensor(out=o[:, t, :], in0=prods[g][t][:, 0:NS], in1=vt[:, i, 0:NS], op=SUB)
+            nc.sync.dma_start(out=out_rows[:, g * GROUP : (g + 1) * GROUP, :], in_=o[:])
+
+        stage_t(0)
+        stage_q(0)
+        stage_t(1)
+        for g in range(n_groups):
+            stage_m(g)
+            if g + 1 < n_groups:
+                stage_q(g + 1)
+            if g + 2 < n_groups:
+                stage_t(g + 2)
+            stage_s(g)
+
+        r0 = const.tile([1, NS], F32, name="r0")
+        v0 = where[0][0]
+        nc.gpsimd.tensor_tensor(out=r0[:], in0=v0[0:1, 0, 0:NS], in1=x0_sb[:], op=SUB)
+        nc.sync.dma_start(out=out[0:NS].rearrange("(o n) -> o n", o=1), in_=r0[:])

@@ -16,7 +16,9 @@ NA = 512
 STEPS = 8192
 J = STEPS // P
 GROUP = 4
-LOAD_CHUNKS = [4, 4, 8, 16, 16, 16]
+LOAD_CHUNKS = [4, 4, 8, 16, 32]
+STORE_CHUNKS = [8, 8, 8, 8, 8, 8, 8, 4, 2, 2]
+OFFLOAD = 0
 FLOPS = 2 * STEPS * NS * NA
 
 
@@ -122,18 +124,41 @@ def tile_constrainnet_t_kernel(tc, A, B, x0, net_input, T, out):
                     )
                 prods[g].append(pr)
 
+        o_where = []
+        j0 = 0
+        for c, n in enumerate(STORE_CHUNKS):
+            ot = opool.tile([P, n, NS], F32, name="o%d" % c)
+            for i in range(n):
+                o_where.append((ot, i, j0, n))
+            j0 += n
+        assert j0 == J
+
+        def stage_c(g):
+            j = g * GROUP + OFFLOAD
+            ot, i, c0, n = o_where[j]
+            nc.scalar.copy(out=ot[:, i, :], in_=prods[g][OFFLOAD][:, 0:NS])
+
         def stage_s(g):
-            o = opool.tile([P, GROUP, NS], F32, name="o%d" % g)
+            for t in [OFFLOAD] + [t for t in range(GROUP) if t != OFFLOAD]:
+                j = g * GROUP + t
+                ot, i, c0, n = o_where[j]
+                vt, vi = where[j + 1]
+                if t == OFFLOAD:
+                    nc.gpsimd.tensor_tensor(out=ot[:, i, :], in0=ot[:, i, :], in1=vt[:, vi, 0:NS], op=SUB)
+                else:
+                    nc.vector.tensor_tensor(out=ot[:, i, :], in0=prods[g][t][:, 0:NS], in1=vt[:, vi, 0:NS], op=SUB)
             for t in range(GROUP):
-                vt, i = where[g * GROUP + t + 1]
-                nc.vector.tensor_tensor(out=o[:, t, :], in0=prods[g][t][:, 0:NS], in1=vt[:, i, 0:NS], op=SUB)
-            nc.sync.dma_start(out=out_rows[:, g * GROUP : (g + 1) * GROUP, :], in_=o[:])
+                j = g * GROUP + t
+                ot, i, c0, n = o_where[j]
+                if i == n - 1:
+                    nc.sync.dma_start(out=out_rows[:, c0 : c0 + n, :], in_=ot[:])
 
         stage_t(0)
         stage_q(0)
         stage_t(1)
         for g in range(n_groups):
             stage_m(g)
+            stage_c(g)
             if g + 1 < n_groups:
                 stage_q(g + 1)
             if g + 2 < n_groups:

@@ -35,9 +35,13 @@ def tile_constrainnet_t_kernel(tc, A, B, x0, net_input, T, out):
         xt_ps = ctx.enter_context(tc.psum_pool(name="xt_ps", bufs=3))
         pr_ps = ctx.enter_context(tc.psum_pool(name="pr_ps", bufs=5))
 
+        ctx.enter_context(tc.manual_schedule())
+
         ident = const.tile([P, P], F32, name="ident")
         make_identity(nc, ident[:])
 
+        x0_sb = const.tile([1, NS], BF16, name="x0_sb")
+        nc.sync.dma_start(out=x0_sb[:], in_=x0.rearrange("(o n) -> o n", o=1))
         ab_sb = const.tile([P, 3, NA], BF16, name="ab_sb")
         nc.sync.dma_start(out=ab_sb[:, :, 0:NS], in_=A.rearrange("(r p) k -> p r k", p=P))
         nc.sync.dma_start(out=ab_sb[:, :, NS:NA], in_=B.rearrange("(r p) k -> p r k", p=P))
@@ -55,8 +59,11 @@ def tile_constrainnet_t_kernel(tc, A, B, x0, net_input, T, out):
         v_last = vpool.tile([P, 1, NS], BF16, name="v_last")
         nc.sync.dma_start(out=v_last[:], in_=v_next[:, J - 1 : J, 0:NS])
         where.append((v_last, 0))
-        x0_sb = const.tile([1, NS], BF16, name="x0_sb")
-        nc.sync.dma_start(out=x0_sb[:], in_=x0.rearrange("(o n) -> o n", o=1))
+
+        r0 = const.tile([1, NS], F32, name="r0")
+        v0 = where[0][0]
+        nc.gpsimd.tensor_tensor(out=r0[:], in0=v0[0:1, 0, 0:NS], in1=x0_sb[:], op=SUB)
+        nc.sync.dma_start(out=out[0:NS].rearrange("(o n) -> o n", o=1), in_=r0[:])
 
         out_rows = out[NS : (STEPS + 1) * NS].rearrange("(p j i) -> p j i", p=P, j=J)
 
@@ -164,8 +171,3 @@ def tile_constrainnet_t_kernel(tc, A, B, x0, net_input, T, out):
             if g + 2 < n_groups:
                 stage_t(g + 2)
             stage_s(g)
-
-        r0 = const.tile([1, NS], F32, name="r0")
-        v0 = where[0][0]
-        nc.gpsimd.tensor_tensor(out=r0[:], in0=v0[0:1, 0, 0:NS], in1=x0_sb[:], op=SUB)
-        nc.sync.dma_start(out=out[0:NS].rearrange("(o n) -> o n", o=1), in_=r0[:])

@@ -79,18 +79,14 @@ def tile_constrainnet_t_kernel(tc, A, B, x0, net_input, T, out):
             )
 
         ab_f = ab_sb[:].bitcast(F32)
-        ab_g = const.tile([P, NS * 4], BF16, name="ab_g", align_bytes=64)
-        ab_gf = ab_g[:].bitcast(F32).rearrange("q (t c u) -> q t c u", t=3, u=2)
-        ab_codes = const.tile([P, NS], U32, name="ab_codes", align_bytes=64)
-        ab_scales = const.tile([P, NS], U8, name="ab_scales", align_bytes=64)
+        ab_g = const.tile([P, 512 * 4], BF16, name="ab_g", align_bytes=64)
+        nc.vector.memset(ab_g[:, NS * 4 : 512 * 4].bitcast(mybir.dt.int32), 0)
+        ab_gf = ab_g[:, 0 : NS * 4].bitcast(F32).rearrange("q (t c u) -> q t c u", t=3, u=2)
+        ab_codes = const.tile([P, 512], U32, name="ab_codes", align_bytes=64)
+        ab_scales = const.tile([P, 512], U8, name="ab_scales", align_bytes=64)
         transpose_pair([ab_f[:, 0, :], ab_f[:, 1, :]], ab_gf[:, 0:2, :, :])
         transpose_pair([ab_f[:, 2, :]], ab_gf[:, 2:3, :, :])
-        nc.vector.quantize_mx(
-            out=ab_codes[:, 0:256].bitcast(FP8X4), scales=ab_scales[:, 0:256], in_=ab_g[:, 0:1024]
-        )
-        nc.vector.quantize_mx(
-            out=ab_codes[:, 256:384].bitcast(FP8X4), scales=ab_scales[:, 256:384], in_=ab_g[:, 1024:1536]
-        )
+        nc.vector.quantize_mx(out=ab_codes[:].bitcast(FP8X4), scales=ab_scales[:], in_=ab_g[:])
 
         grouped = {}
         quant = {}
@@ -119,7 +115,7 @@ def tile_constrainnet_t_kernel(tc, A, B, x0, net_input, T, out):
             for t in range(GROUP):
                 pr = pr_ps.tile([P, 512], F32, name="pr")
                 cols = slice(t * P, (t + 1) * P)
-                for lo, hi in ((0, 256), (256, 384)):
+                for lo, hi in ((0, 512),):
                     nc.tensor.matmul_mx(
                         out=pr[:, lo:hi],
                         lhsT=codes[:, cols].bitcast(FP8X4),

@@ -18,7 +18,7 @@ J = STEPS // P
 GROUP = 4
 LOAD_CHUNKS = [4, 4, 8, 16, 32]
 STORE_CHUNKS = [8, 8, 8, 8, 8, 8, 8, 4, 2, 2]
-OFFLOAD = 0
+OFFLOAD = -1
 FLOPS = 2 * STEPS * NS * NA
 
 
@@ -79,14 +79,18 @@ def tile_constrainnet_t_kernel(tc, A, B, x0, net_input, T, out):
             )
 
         ab_f = ab_sb[:].bitcast(F32)
-        ab_g = const.tile([P, 512 * 4], BF16, name="ab_g", align_bytes=64)
-        nc.vector.memset(ab_g[:, NS * 4 : 512 * 4].bitcast(mybir.dt.int32), 0)
-        ab_gf = ab_g[:, 0 : NS * 4].bitcast(F32).rearrange("q (t c u) -> q t c u", t=3, u=2)
-        ab_codes = const.tile([P, 512], U32, name="ab_codes", align_bytes=64)
-        ab_scales = const.tile([P, 512], U8, name="ab_scales", align_bytes=64)
+        ab_g = const.tile([P, NS * 4], BF16, name="ab_g", align_bytes=64)
+        ab_gf = ab_g[:].bitcast(F32).rearrange("q (t c u) -> q t c u", t=3, u=2)
+        ab_codes = const.tile([P, NS], U32, name="ab_codes", align_bytes=64)
+        ab_scales = const.tile([P, NS], U8, name="ab_scales", align_bytes=64)
         transpose_pair([ab_f[:, 0, :], ab_f[:, 1, :]], ab_gf[:, 0:2, :, :])
         transpose_pair([ab_f[:, 2, :]], ab_gf[:, 2:3, :, :])
-        nc.vector.quantize_mx(out=ab_codes[:].bitcast(FP8X4), scales=ab_scales[:], in_=ab_g[:])
+        nc.vector.quantize_mx(
+            out=ab_codes[:, 0:256].bitcast(FP8X4), scales=ab_scales[:, 0:256], in_=ab_g[:, 0:1024]
+        )
+        nc.vector.quantize_mx(
+            out=ab_codes[:, 256:384].bitcast(FP8X4), scales=ab_scales[:, 256:384], in_=ab_g[:, 1024:1536]
+        )
 
         grouped = {}
         quant = {}
@@ -115,7 +119,7 @@ def tile_constrainnet_t_kernel(tc, A, B, x0, net_input, T, out):
             for t in range(GROUP):
                 pr = pr_ps.tile([P, 512], F32, name="pr")
                 cols = slice(t * P, (t + 1) * P)
-                for lo, hi in ((0, 512),):
+                for lo, hi in ((0, 256), (256, 384)):
                     nc.tensor.matmul_mx(
                         out=pr[:, lo:hi],
                         lhsT=codes[:, cols].bitcast(FP8X4),
@@ -142,7 +146,7 @@ def tile_constrainnet_t_kernel(tc, A, B, x0, net_input, T, out):
             nc.scalar.copy(out=ot[:, i, :], in_=prods[g][OFFLOAD][:, 0:NS])
 
         def stage_s(g):
-            for t in [OFFLOAD] + [t for t in range(GROUP) if t != OFFLOAD]:
+            for t in range(GROUP):
                 j = g * GROUP + t
                 ot, i, c0, n = o_where[j]
                 vt, vi = where[j + 1]
@@ -161,7 +165,6 @@ def tile_constrainnet_t_kernel(tc, A, B, x0, net_input, T, out):
         stage_t(1)
         for g in range(n_groups):
             stage_m(g)
-            stage_c(g)
             if g + 1 < n_groups:
                 stage_q(g + 1)
             if g + 2 < n_groups:

@@ -13,19 +13,22 @@ SUB = mybir.AluOpType.subtract
 P = 128
 NS = 384
 NA = 512
+PACK = 4
 STEPS = 8192
-J = STEPS // P
+SLOTS = STEPS // P
 GROUP = 4
-LOAD_CHUNKS = [4, 4, 8, 16, 32]
-STORE_CHUNKS = [8, 8, 8, 8, 8, 8, 8, 4, 2, 2]
-OFFLOAD = -1
+BANK = 512
+STATE_SPLITS = ((0, 256), (256, NS))
+LOAD_SLOTS = [4, 4, 8, 16, 32]
+STORE_SLOTS = 2 * GROUP
 FLOPS = 2 * STEPS * NS * NA
 
 
 def tile_constrainnet_t_kernel(tc, A, B, x0, net_input, T, out):
     nc = tc.nc
     assert T == STEPS + 1
-    n_groups = J // GROUP
+    assert sum(LOAD_SLOTS) == SLOTS and SLOTS % STORE_SLOTS == 0
+    n_groups = SLOTS // GROUP
     with ExitStack() as ctx:
         const = ctx.enter_context(tc.tile_pool(name="const", bufs=1))
         vpool = ctx.enter_context(tc.tile_pool(name="vpool", bufs=1))
@@ -42,131 +45,121 @@ def tile_constrainnet_t_kernel(tc, A, B, x0, net_input, T, out):
 
         x0_sb = const.tile([1, NS], BF16, name="x0_sb")
         nc.sync.dma_start(out=x0_sb[:], in_=x0.rearrange("(o n) -> o n", o=1))
-        ab_sb = const.tile([P, 3, NA], BF16, name="ab_sb")
+        ab_sb = const.tile([P, NS // P, NA], BF16, name="ab_sb")
         nc.sync.dma_start(out=ab_sb[:, :, 0:NS], in_=A.rearrange("(r p) k -> p r k", p=P))
         nc.sync.dma_start(out=ab_sb[:, :, NS:NA], in_=B.rearrange("(r p) k -> p r k", p=P))
-        v_rows = net_input[0 : STEPS * NA].rearrange("(p j k) -> p j k", p=P, j=J)
-        where = []
-        j0 = 0
-        for c, n in enumerate(LOAD_CHUNKS):
-            vt = vpool.tile([P, n, NA], BF16, name="v%d" % c)
-            nc.sync.dma_start(out=vt[:], in_=v_rows[:, j0 : j0 + n, :])
+        v_slots = net_input[0 : STEPS * NA].rearrange("(p j k) -> p j k", p=P, j=SLOTS)
+        v_of_slot = []
+        first = 0
+        for c, n in enumerate(LOAD_SLOTS):
+            v_sb = vpool.tile([P, n, NA], BF16, name="v%d" % c)
+            nc.sync.dma_start(out=v_sb[:], in_=v_slots[:, first : first + n, :])
             for i in range(n):
-                where.append((vt, i))
-            j0 += n
-        assert j0 == J
-        v_next = net_input[NA : (STEPS + 1) * NA].rearrange("(p j k) -> p j k", p=P, j=J)
+                v_of_slot.append((v_sb, i))
+            first += n
+        v_shifted = net_input[NA : (STEPS + 1) * NA].rearrange("(p j k) -> p j k", p=P, j=SLOTS)
         v_last = vpool.tile([P, 1, NS], BF16, name="v_last")
-        nc.sync.dma_start(out=v_last[:], in_=v_next[:, J - 1 : J, 0:NS])
-        where.append((v_last, 0))
+        nc.sync.dma_start(out=v_last[:], in_=v_shifted[:, SLOTS - 1 : SLOTS, 0:NS])
+        v_of_slot.append((v_last, 0))
 
         r0 = const.tile([1, NS], F32, name="r0")
-        v0 = where[0][0]
-        nc.gpsimd.tensor_tensor(out=r0[:], in0=v0[0:1, 0, 0:NS], in1=x0_sb[:], op=SUB)
+        nc.gpsimd.tensor_tensor(out=r0[:], in0=v_of_slot[0][0][0:1, 0, 0:NS], in1=x0_sb[:], op=SUB)
         nc.sync.dma_start(out=out[0:NS].rearrange("(o n) -> o n", o=1), in_=r0[:])
 
-        out_rows = out[NS : (STEPS + 1) * NS].rearrange("(p j i) -> p j i", p=P, j=J)
+        r_slots = out[NS : (STEPS + 1) * NS].rearrange("(p j i) -> p j i", p=P, j=SLOTS)
 
-        def transpose_pair(srcs, dst_f32):
-            xt = xt_ps.tile([P, 4, P], F32, name="xt")
-            n = len(srcs)
-            for t, s in enumerate(srcs):
+        def k_to_partitions(rows, grouped_words):
+            xt = xt_ps.tile([P, BANK // P, P], F32, name="xt")
+            for b, words in enumerate(rows):
                 for u in range(2):
-                    nc.tensor.transpose(xt[:, 2 * t + u, :], s[:, u * P : (u + 1) * P], ident[:])
+                    nc.tensor.transpose(xt[:, 2 * b + u, :], words[:, u * P : (u + 1) * P], ident[:])
             nc.scalar.copy(
-                out=dst_f32,
-                in_=xt[:, 0 : 2 * n, :].rearrange("q (t u) c -> q t c u", u=2),
+                out=grouped_words,
+                in_=xt[:, 0 : 2 * len(rows), :].rearrange("q (b u) r -> q b r u", u=2),
             )
 
-        ab_f = ab_sb[:].bitcast(F32)
-        ab_g = const.tile([P, NS * 4], BF16, name="ab_g", align_bytes=64)
-        ab_gf = ab_g[:].bitcast(F32).rearrange("q (t c u) -> q t c u", t=3, u=2)
+        ab_words = ab_sb[:].bitcast(F32)
+        ab_g = const.tile([P, NS * PACK], BF16, name="ab_g", align_bytes=64)
+        ab_g_words = ab_g[:].bitcast(F32).rearrange("q (b r u) -> q b r u", b=NS // P, u=2)
         ab_codes = const.tile([P, NS], U32, name="ab_codes", align_bytes=64)
         ab_scales = const.tile([P, NS], U8, name="ab_scales", align_bytes=64)
-        transpose_pair([ab_f[:, 0, :], ab_f[:, 1, :]], ab_gf[:, 0:2, :, :])
-        transpose_pair([ab_f[:, 2, :]], ab_gf[:, 2:3, :, :])
-        nc.vector.quantize_mx(
-            out=ab_codes[:, 0:256].bitcast(FP8X4), scales=ab_scales[:, 0:256], in_=ab_g[:, 0:1024]
-        )
-        nc.vector.quantize_mx(
-            out=ab_codes[:, 256:384].bitcast(FP8X4), scales=ab_scales[:, 256:384], in_=ab_g[:, 1024:1536]
-        )
+        k_to_partitions([ab_words[:, 0, :], ab_words[:, 1, :]], ab_g_words[:, 0:2, :, :])
+        k_to_partitions([ab_words[:, 2, :]], ab_g_words[:, 2:3, :, :])
+        for lo, hi in STATE_SPLITS:
+            nc.vector.quantize_mx(
+                out=ab_codes[:, lo:hi].bitcast(FP8X4),
+                scales=ab_scales[:, lo:hi],
+                in_=ab_g[:, lo * PACK : hi * PACK],
+            )
+
+        r_tiles = [opool.tile([P, STORE_SLOTS, NS], F32, name="o%d" % c) for c in range(SLOTS // STORE_SLOTS)]
+
+        def result_of(j):
+            return r_tiles[j // STORE_SLOTS][:, j % STORE_SLOTS, :]
 
         grouped = {}
-        quant = {}
-        prods = {}
+        quantised = {}
+        products = {}
 
-        def stage_t(g):
-            gr = gpool.tile([P, GROUP * 4 * P], BF16, name="gr", align_bytes=64)
-            grf = gr[:].bitcast(F32).rearrange("q (t c u) -> q t c u", t=GROUP, u=2)
+        def regroup(g):
+            gr = gpool.tile([P, GROUP * P * PACK], BF16, name="gr", align_bytes=64)
+            gr_words = gr[:].bitcast(F32).rearrange("q (b r u) -> q b r u", b=GROUP, u=2)
             for h in range(GROUP // 2):
-                srcs = []
-                for t in range(2):
-                    vt, i = where[g * GROUP + 2 * h + t]
-                    srcs.append(vt[:].bitcast(F32)[:, i, :])
-                transpose_pair(srcs, grf[:, 2 * h : 2 * h + 2, :, :])
+                rows = []
+                for b in range(2):
+                    v_sb, i = v_of_slot[g * GROUP + 2 * h + b]
+                    rows.append(v_sb[:].bitcast(F32)[:, i, :])
+                k_to_partitions(rows, gr_words[:, 2 * h : 2 * h + 2, :, :])
             grouped[g] = gr
 
-        def stage_q(g):
+        def quantise(g):
             codes = qpool.tile([P, GROUP * P], U32, name="codes", align_bytes=64)
             scales = qpool.tile([P, GROUP * P], U8, name="scales", align_bytes=64)
             nc.vector.quantize_mx(out=codes[:].bitcast(FP8X4), scales=scales[:], in_=grouped[g][:])
-            quant[g] = (codes, scales)
+            quantised[g] = (codes, scales)
 
-        def stage_m(g):
-            codes, scales = quant[g]
-            prods[g] = []
-            for t in range(GROUP):
-                pr = pr_ps.tile([P, 512], F32, name="pr")
-                cols = slice(t * P, (t + 1) * P)
-                for lo, hi in ((0, 256), (256, 384)):
+        def multiply(g):
+            codes, scales = quantised[g]
+            products[g] = []
+            for b in range(GROUP):
+                pr = pr_ps.tile([P, BANK], F32, name="pr")
+                steps = slice(b * P, (b + 1) * P)
+                for lo, hi in STATE_SPLITS:
                     nc.tensor.matmul_mx(
                         out=pr[:, lo:hi],
-                        lhsT=codes[:, cols].bitcast(FP8X4),
-                        lhsT_scale=scales[:, cols],
+                        lhsT=codes[:, steps].bitcast(FP8X4),
+                        lhsT_scale=scales[:, steps],
                         rhs=ab_codes[:, lo:hi].bitcast(FP8X4),
                         rhs_scale=ab_scales[:, lo:hi],
                         start=True,
                         stop=True,
                     )
-                prods[g].append(pr)
+                products[g].append(pr)
 
-        o_where = []
-        j0 = 0
-        for c, n in enumerate(STORE_CHUNKS):
-            ot = opool.tile([P, n, NS], F32, name="o%d" % c)
-            for i in range(n):
-                o_where.append((ot, i, j0, n))
-            j0 += n
-        assert j0 == J
+        def copy_first_product(g):
+            nc.scalar.copy(out=result_of(g * GROUP), in_=products[g][0][:, 0:NS])
 
-        def stage_c(g):
-            j = g * GROUP + OFFLOAD
-            ot, i, c0, n = o_where[j]
-            nc.scalar.copy(out=ot[:, i, :], in_=prods[g][OFFLOAD][:, 0:NS])
-
-        def stage_s(g):
-            for t in range(GROUP):
-                j = g * GROUP + t
-                ot, i, c0, n = o_where[j]
-                vt, vi = where[j + 1]
-                if t == OFFLOAD:
-                    nc.gpsimd.tensor_tensor(out=ot[:, i, :], in0=ot[:, i, :], in1=vt[:, vi, 0:NS], op=SUB)
+        def subtract_and_store(g):
+            for b in range(GROUP):
+                j = g * GROUP + b
+                v_sb, i = v_of_slot[j + 1]
+                x_next = v_sb[:, i, 0:NS]
+                if b == 0:
+                    nc.gpsimd.tensor_tensor(out=result_of(j), in0=result_of(j), in1=x_next, op=SUB)
                 else:
-                    nc.vector.tensor_tensor(out=ot[:, i, :], in0=prods[g][t][:, 0:NS], in1=vt[:, vi, 0:NS], op=SUB)
-            for t in range(GROUP):
-                j = g * GROUP + t
-                ot, i, c0, n = o_where[j]
-                if i == n - 1:
-                    nc.sync.dma_start(out=out_rows[:, c0 : c0 + n, :], in_=ot[:])
+                    nc.vector.tensor_tensor(out=result_of(j), in0=products[g][b][:, 0:NS], in1=x_next, op=SUB)
+            done = (g + 1) * GROUP
+            if done % STORE_SLOTS == 0:
+                nc.sync.dma_start(out=r_slots[:, done - STORE_SLOTS : done, :], in_=r_tiles[done // STORE_SLOTS - 1][:])
 
-        stage_t(0)
-        stage_q(0)
-        stage_t(1)
+        regroup(0)
+        quantise(0)
+        regroup(1)
         for g in range(n_groups):
-            stage_m(g)
+            multiply(g)
+            copy_first_product(g)
             if g + 1 < n_groups:
-                stage_q(g + 1)
+                quantise(g + 1)
             if g + 2 < n_groups:
-                stage_t(g + 2)
-            stage_s(g)
+                regroup(g + 2)
+            subtract_and_store(g)

from contextlib import ExitStack

import concourse.mybir as mybir
from concourse.masks import make_identity

F32 = mybir.dt.float32
BF16 = mybir.dt.bfloat16
U32 = mybir.dt.uint32
U8 = mybir.dt.uint8
FP8X4 = mybir.dt.float8_e4m3fn_x4
SUB = mybir.AluOpType.subtract

P = 128
NS = 384
NA = 512
PACK = 4
STEPS = 8192
SLOTS = STEPS // P
GROUP = 4
BANK = 512
STATE_SPLITS = ((0, 256), (256, NS))
LOAD_SLOTS = [4, 4, 8, 16, 32]
STORE_SLOTS = 2 * GROUP
FLOPS = 2 * STEPS * NS * NA


def tile_constrainnet_t_kernel(tc, A, B, x0, net_input, T, out):
    nc = tc.nc
    assert T == STEPS + 1
    assert sum(LOAD_SLOTS) == SLOTS and SLOTS % STORE_SLOTS == 0
    n_groups = SLOTS // GROUP
    with ExitStack() as ctx:
        const = ctx.enter_context(tc.tile_pool(name="const", bufs=1))
        vpool = ctx.enter_context(tc.tile_pool(name="vpool", bufs=1))
        opool = ctx.enter_context(tc.tile_pool(name="opool", bufs=1))
        gpool = ctx.enter_context(tc.tile_pool(name="gpool", bufs=3))
        qpool = ctx.enter_context(tc.tile_pool(name="qpool", bufs=3))
        xt_ps = ctx.enter_context(tc.psum_pool(name="xt_ps", bufs=3))
        pr_ps = ctx.enter_context(tc.psum_pool(name="pr_ps", bufs=5))

        ctx.enter_context(tc.manual_schedule())

        ident = const.tile([P, P], F32, name="ident")
        make_identity(nc, ident[:])

        x0_sb = const.tile([1, NS], BF16, name="x0_sb")
        nc.sync.dma_start(out=x0_sb[:], in_=x0.rearrange("(o n) -> o n", o=1))
        ab_sb = const.tile([P, NS // P, NA], BF16, name="ab_sb")
        nc.sync.dma_start(out=ab_sb[:, :, 0:NS], in_=A.rearrange("(r p) k -> p r k", p=P))
        nc.sync.dma_start(out=ab_sb[:, :, NS:NA], in_=B.rearrange("(r p) k -> p r k", p=P))
        v_slots = net_input[0 : STEPS * NA].rearrange("(p j k) -> p j k", p=P, j=SLOTS)
        v_of_slot = []
        first = 0
        for c, n in enumerate(LOAD_SLOTS):
            v_sb = vpool.tile([P, n, NA], BF16, name="v%d" % c)
            nc.sync.dma_start(out=v_sb[:], in_=v_slots[:, first : first + n, :])
            for i in range(n):
                v_of_slot.append((v_sb, i))
            first += n
        v_shifted = net_input[NA : (STEPS + 1) * NA].rearrange("(p j k) -> p j k", p=P, j=SLOTS)
        v_last = vpool.tile([P, 1, NS], BF16, name="v_last")
        nc.sync.dma_start(out=v_last[:], in_=v_shifted[:, SLOTS - 1 : SLOTS, 0:NS])
        v_of_slot.append((v_last, 0))

        r0 = const.tile([1, NS], F32, name="r0")
        nc.gpsimd.tensor_tensor(out=r0[:], in0=v_of_slot[0][0][0:1, 0, 0:NS], in1=x0_sb[:], op=SUB)
        nc.sync.dma_start(out=out[0:NS].rearrange("(o n) -> o n", o=1), in_=r0[:])

        r_slots = out[NS : (STEPS + 1) * NS].rearrange("(p j i) -> p j i", p=P, j=SLOTS)

        def k_to_partitions(rows, grouped_words):
            xt = xt_ps.tile([P, BANK // P, P], F32, name="xt")
            for b, words in enumerate(rows):
                for u in range(2):
                    nc.tensor.transpose(xt[:, 2 * b + u, :], words[:, u * P : (u + 1) * P], ident[:])
            nc.scalar.copy(
                out=grouped_words,
                in_=xt[:, 0 : 2 * len(rows), :].rearrange("q (b u) r -> q b r u", u=2),
            )

        ab_words = ab_sb[:].bitcast(F32)
        ab_g = const.tile([P, NS * PACK], BF16, name="ab_g", align_bytes=64)
        ab_g_words = ab_g[:].bitcast(F32).rearrange("q (b r u) -> q b r u", b=NS // P, u=2)
        ab_codes = const.tile([P, NS], U32, name="ab_codes", align_bytes=64)
        ab_scales = const.tile([P, NS], U8, name="ab_scales", align_bytes=64)
        k_to_partitions([ab_words[:, 0, :], ab_words[:, 1, :]], ab_g_words[:, 0:2, :, :])
        k_to_partitions([ab_words[:, 2, :]], ab_g_words[:, 2:3, :, :])
        for lo, hi in STATE_SPLITS:
            nc.vector.quantize_mx(
                out=ab_codes[:, lo:hi].bitcast(FP8X4),
                scales=ab_scales[:, lo:hi],
                in_=ab_g[:, lo * PACK : hi * PACK],
            )

        r_tiles = [opool.tile([P, STORE_SLOTS, NS], F32, name="o%d" % c) for c in range(SLOTS // STORE_SLOTS)]

        def result_of(j):
            return r_tiles[j // STORE_SLOTS][:, j % STORE_SLOTS, :]

        grouped = {}
        quantised = {}
        products = {}

        def regroup(g):
            gr = gpool.tile([P, GROUP * P * PACK], BF16, name="gr", align_bytes=64)
            gr_words = gr[:].bitcast(F32).rearrange("q (b r u) -> q b r u", b=GROUP, u=2)
            for h in range(GROUP // 2):
                rows = []
                for b in range(2):
                    v_sb, i = v_of_slot[g * GROUP + 2 * h + b]
                    rows.append(v_sb[:].bitcast(F32)[:, i, :])
                k_to_partitions(rows, gr_words[:, 2 * h : 2 * h + 2, :, :])
            grouped[g] = gr

        def quantise(g):
            codes = qpool.tile([P, GROUP * P], U32, name="codes", align_bytes=64)
            scales = qpool.tile([P, GROUP * P], U8, name="scales", align_bytes=64)
            nc.vector.quantize_mx(out=codes[:].bitcast(FP8X4), scales=scales[:], in_=grouped[g][:])
            quantised[g] = (codes, scales)

        def multiply(g):
            codes, scales = quantised[g]
            products[g] = []
            for b in range(GROUP):
                pr = pr_ps.tile([P, BANK], F32, name="pr")
                steps = slice(b * P, (b + 1) * P)
                for lo, hi in STATE_SPLITS:
                    nc.tensor.matmul_mx(
                        out=pr[:, lo:hi],
                        lhsT=codes[:, steps].bitcast(FP8X4),
                        lhsT_scale=scales[:, steps],
                        rhs=ab_codes[:, lo:hi].bitcast(FP8X4),
                        rhs_scale=ab_scales[:, lo:hi],
                        start=True,
                        stop=True,
                    )
                products[g].append(pr)

        def copy_first_product(g):
            nc.scalar.copy(out=result_of(g * GROUP), in_=products[g][0][:, 0:NS])

        def subtract_and_store(g):
            for b in range(GROUP):
                j = g * GROUP + b
                v_sb, i = v_of_slot[j + 1]
                x_next = v_sb[:, i, 0:NS]
                if b == 0:
                    nc.gpsimd.tensor_tensor(out=result_of(j), in0=result_of(j), in1=x_next, op=SUB)
                else:
                    nc.vector.tensor_tensor(out=result_of(j), in0=products[g][b][:, 0:NS], in1=x_next, op=SUB)
            done = (g + 1) * GROUP
            if done % STORE_SLOTS == 0:
                nc.sync.dma_start(out=r_slots[:, done - STORE_SLOTS : done, :], in_=r_tiles[done // STORE_SLOTS - 1][:])

        regroup(0)
        quantise(0)
        regroup(1)
        for g in range(n_groups):
            multiply(g)
            copy_first_product(g)
            if g + 1 < n_groups:
                quantise(g + 1)
            if g + 2 < n_groups:
                regroup(g + 2)
            subtract_and_store(g)
